import numpy as np
import ml_dtypes


def mxq(x, axis, fmt="e4m3"):
    dtype, down = {"e4m3": (ml_dtypes.float8_e4m3fn, 7), "e5m2": (ml_dtypes.float8_e5m2, 14)}[fmt]
    v = np.moveaxis(np.asarray(x, np.float32).astype(ml_dtypes.bfloat16).astype(np.float64), axis, -1)
    blocks = v.reshape(v.shape[:-1] + (-1, 32))
    amax = np.abs(blocks).max(-1, keepdims=True)
    byte = np.maximum(np.where(amax > 0, np.frexp(amax)[1] - 1 + 127, 0) - down, 1)
    scale = np.exp2(byte - 127.0)
    codes = (blocks / scale).astype(np.float32).astype(dtype).astype(np.float64)
    return np.moveaxis((codes * scale).reshape(v.shape), -1, axis)


WIDE = False


def mx_kscale(k):
    if not WIDE:
        return np.ones(k)
    levels = np.array([10, -10, 5, -5, 0])
    if k % 512:
        return np.exp2(np.random.permutation(np.resize(levels, k // 32))).repeat(32)
    a = np.empty((k // 512, 16))
    for p in range(k // 512):
        a[p, :8] = np.random.permutation(np.resize(levels, 8))
        for g in range(8):
            far = levels[np.abs(levels - a[p, g]) >= 10]
            a[p, g + 8] = far[np.random.randint(len(far))]
    return np.exp2(a.ravel()).repeat(32)


BF16 = ml_dtypes.bfloat16


def bf(x):
    return np.asarray(x, np.float32).astype(BF16)


def f64(x):
    return np.asarray(x).astype(np.float64)


B, S, HID, NH, HD, RD, RATIO = 1, 2048, 1024, 8, 128, 64, 4
THETA = 10000.0
HALF = RD // 2


def rope_tables(positions):
    inv_freq = 1.0 / THETA ** (np.arange(HALF) / HALF)
    ang = positions[:, None] * inv_freq[None, :]
    return np.cos(ang), np.sin(ang)


def rope_interleaved(x, cos, sin):
    nope, rope = x[..., :-RD], x[..., -RD:]
    pr = rope.reshape(rope.shape[:-1] + (HALF, 2))
    a, b = pr[..., 0], pr[..., 1]
    new = np.stack([a * cos - b * sin, a * sin + b * cos], axis=-1).reshape(rope.shape)
    return np.concatenate([nope, new], axis=-1)


def setup_inputs():
    s = mx_kscale(HID)
    return {"hidden": bf(np.random.standard_normal((B, S, HID)) * s),
            "wq": bf(np.random.standard_normal((HID, NH * HD)) / np.sqrt(HID) / s[:, None])}


def core(hidden, wq):
    q = mxq(f64(hidden), 2, "e4m3") @ mxq(f64(wq), 0, "e4m3")
    q = q.reshape(B, S, NH, HD).transpose(0, 2, 1, 3)
    cq, sq = rope_tables(np.arange(S))
    return rope_interleaved(q, cq, sq)


def e4m3fn_bytes(y):
    return np.clip(np.asarray(y, np.float64), -448.0, 448.0).astype(np.float32).astype(ml_dtypes.float8_e4m3fn).view(np.uint8)


def reference(hidden, wq):
    out = core(hidden, wq)
    s = np.max(np.abs(out), axis=-1, keepdims=True) / 448.0
    return out, e4m3fn_bytes(out / s)

@@ -1,0 +1,279 @@
+from contextlib import ExitStack
+
+import concourse.mybir as mybir
+from concourse.masks import make_identity
+
+FLOPS = 2 * 2048 * 1024 * 1024
+
+F32 = mybir.dt.float32
+BF16 = mybir.dt.bfloat16
+U32 = mybir.dt.uint32
+I32 = mybir.dt.int32
+U8 = mybir.dt.uint8
+FP8X4 = mybir.dt.float8_e4m3fn_x4
+FP8 = mybir.dt.float8_e4m3fn
+ALU = mybir.AluOpType
+ACT = mybir.ActivationFunctionType
+AX = mybir.AxisListType
+
+P = 128
+NOPE = 0
+ROPE = 1
+FREQ_RATIO = 10000.0 ** (-1.0 / 32.0)
+PI = 3.141592653589793
+TWO_PI_HI = 6.28125
+TWO_PI_LO = 2.0 * PI - TWO_PI_HI
+
+
+def tile_deepseekv4attention_pb_kernel(tc, hidden, wq, out_0, out_1):
+    nc = tc.nc
+    with ExitStack() as ctx:
+        const = ctx.enter_context(tc.tile_pool(name="const", bufs=1))
+        work = ctx.enter_context(tc.tile_pool(name="work", bufs=3))
+        psum = ctx.enter_context(tc.psum_pool(name="psum", bufs=2))
+
+        hid = hidden.rearrange("b (s p i) k -> (b s) p i k", p=P, i=4)
+        x_raw = []
+        w_raw = [[None, None], [None, None]]
+
+        def load_x(m):
+            xr = const.tile([P, 2, 1024], BF16, name="x_raw%d" % m, tag="x_raw%d" % m)
+            nc.sync.dma_start(out=xr[:], in_=hid[m // 2, :, 2 * (m % 2) : 2 * (m % 2) + 2, :])
+            x_raw.append(xr)
+
+        def load_w(g, ch):
+            wr = const.tile([P, 4, 512], BF16, name="w_raw%d%d" % (g, ch), tag="w_raw%d%d" % (g, ch))
+            nc.sync.dma_start(
+                out=wr[:],
+                in_=wq[512 * g : 512 * (g + 1), 512 * ch : 512 * (ch + 1)].rearrange("(q j) n -> q j n", j=4),
+            )
+            w_raw[g][ch] = wr
+
+        load_x(0)
+        load_w(0, 0)
+        load_w(0, 1)
+        load_w(1, 0)
+        load_w(1, 1)
+        for m in range(1, 8):
+            load_x(m)
+
+        zero = const.tile([P, 1], F32, name="zero", tag="zero")
+        warm = const.tile([P, 1], F32, name="warm", tag="warm")
+        ident = const.tile([P, P], F32, name="ident", tag="ident")
+        tpos = const.tile([P, 16], F32, name="tpos", tag="tpos")
+        freq = const.tile([P, 32], F32, name="freq", tag="freq")
+        ang = const.tile([P, 16, 32], F32, name="ang", tag="ang")
+        turns = const.tile([P, 16, 32], I32, name="turns", tag="turns")
+        red1 = const.tile([P, 16, 32], F32, name="red1", tag="red1")
+        red2 = const.tile([P, 16, 32], F32, name="red2", tag="red2")
+        half_sin = const.tile([P, 2, 16, 32], F32, name="half_sin", tag="half_sin")
+        half_sq = const.tile([P, 2, 16, 32], F32, name="half_sq", tag="half_sq")
+        cos_t = const.tile([P, 16, 32], F32, name="cos_t", tag="cos_t")
+        sin_t = const.tile([P, 16, 2, 32], F32, name="sin_t", tag="sin_t")
+
+        def frequencies():
+            nc.vector.memset(freq[:, 0:1], 1.0)
+            for b in range(5):
+                n = 1 << b
+                nc.vector.tensor_scalar(out=freq[:, n : 2 * n], in0=freq[:, 0:n], scalar1=FREQ_RATIO ** n,
+                                        scalar2=None, op0=ALU.mult)
+
+        def reduced_angles(c0, c1):
+            cs = slice(c0, c1)
+            nc.vector.tensor_tensor(out=ang[:, cs, :], in0=tpos[:, cs].unsqueeze(2).to_broadcast([P, c1 - c0, 32]),
+                                    in1=freq[:].unsqueeze(1).to_broadcast([P, c1 - c0, 32]), op=ALU.mult)
+            nc.vector.tensor_scalar(out=turns[:, cs, :], in0=ang[:, cs, :], scalar1=1.0 / (2.0 * PI), scalar2=None,
+                                    op0=ALU.mult)
+            nc.vector.scalar_tensor_tensor(out=red1[:, cs, :], in0=turns[:, cs, :], scalar=-TWO_PI_HI,
+                                           in1=ang[:, cs, :], op0=ALU.mult, op1=ALU.add)
+            nc.vector.scalar_tensor_tensor(out=red2[:, cs, :], in0=turns[:, cs, :], scalar=-TWO_PI_LO,
+                                           in1=red1[:, cs, :], op0=ALU.mult, op1=ALU.add)
+
+        def cos_sin(c0, c1):
+            cs = slice(c0, c1)
+            for ph in range(2):
+                nc.scalar.activation(out=half_sin[:, ph, cs, :], in_=red2[:, cs, :], func=ACT.Sin,
+                                     bias=-0.25 * PI * ph, scale=0.5)
+            nc.scalar.activation(out=half_sq[:, 0, cs, :], in_=half_sin[:, 0, cs, :], func=ACT.Square)
+            nc.scalar.activation(out=cos_t[:, cs, :], in_=half_sq[:, 0, cs, :], func=ACT.Copy, bias=1.0, scale=-2.0)
+            nc.scalar.activation(out=half_sq[:, 1, cs, :], in_=half_sin[:, 1, cs, :], func=ACT.Square)
+            nc.scalar.activation(out=sin_t[:, cs, 0, :], in_=half_sq[:, 1, cs, :], func=ACT.Copy, bias=-1.0, scale=2.0)
+            nc.scalar.activation(out=sin_t[:, cs, 1, :], in_=half_sq[:, 1, cs, :], func=ACT.Copy, bias=1.0, scale=-2.0)
+
+        x_grp = {}
+        x_code = {}
+        x_scale = {}
+
+        def transpose_pair(m):
+            xg = work.tile([P, 2, 2, P, 4], BF16, name="x_grp", tag="x_grp", bufs=3, align_bytes=64)
+            for a in range(2):
+                words = x_raw[m][:, a, :].bitcast(F32)
+                xt = psum.tile([P, 2, 2, P], F32, name="xt", tag="xt", bufs=2)
+                for g in range(2):
+                    for u in range(2):
+                        nc.tensor.transpose(xt[:, g, u, :], words[:, 256 * g + u : 256 * (g + 1) : 2], ident[:])
+                nc.scalar.copy(out=xg[:, a].bitcast(F32), in_=xt[:].rearrange("q g u p -> q g p u"))
+            x_grp[m] = xg
+
+        def quant_pair(m):
+            xc = work.tile([P, 512], U32, name="x_code", tag="x_code", bufs=4, align_bytes=64)
+            xs = work.tile([P, 512], U8, name="x_scale", tag="x_scale", bufs=4, align_bytes=64)
+            nc.vector.quantize_mx(out=xc[:].bitcast(FP8X4), scales=xs[:],
+                                  in_=x_grp[m][:].rearrange("q a g p t -> q (a g p t)"))
+            x_code[m] = xc
+            x_scale[m] = xs
+
+        w_grp = [[None, None], [None, None]]
+        w_code = [[None, None], [None, None]]
+        w_scale = [[None, None], [None, None]]
+
+        def interleave_w(g):
+            for t in (ROPE, NOPE):
+                w_grp[g][t] = const.tile([P, 512, 4], BF16, name="w_grp%d%d" % (g, t), tag="w_grp%d%d" % (g, t),
+                                         align_bytes=64)
+            for ch in range(2):
+                cols = slice(256 * ch, 256 * (ch + 1))
+                nc.vector.tensor_copy(
+                    out=w_grp[g][ROPE][:, cols, :].rearrange("q (h d) j -> q h d j", h=4),
+                    in_=w_raw[g][ch][:].rearrange("q j (h t d) -> q t h d j", h=4, t=2)[:, ROPE],
+                )
+                nc.scalar.copy(
+                    out=w_grp[g][NOPE][:, cols, :].rearrange("q (h d) j -> q h d j", h=4),
+                    in_=w_raw[g][ch][:].rearrange("q j (h t d) -> q t h d j", h=4, t=2)[:, NOPE],
+                )
+
+        def quant_w(g, t):
+            wc = const.tile([P, 512], U32, name="w_code%d%d" % (g, t), tag="w_code%d%d" % (g, t), align_bytes=64)
+            ws = const.tile([P, 512], U8, name="w_scale%d%d" % (g, t), tag="w_scale%d%d" % (g, t), align_bytes=64)
+            nc.vector.quantize_mx(out=wc[:].bitcast(FP8X4), scales=ws[:],
+                                  in_=w_grp[g][t][:].rearrange("q n j -> q (n j)"))
+            w_code[g][t] = wc
+            w_scale[g][t] = ws
+
+        acc = {}
+        o_tiles = {}
+
+        def mm(tau, t):
+            m, a = tau // 2, tau % 2
+            ps = psum.tile([P, 512], F32, name="acc%d" % t, tag="acc%d" % t, bufs=3)
+            for g in range(2):
+                cols = slice(256 * a + 128 * g, 256 * a + 128 * (g + 1))
+                nc.tensor.matmul_mx(out=ps[:], lhsT=x_code[m][:, cols].bitcast(FP8X4),
+                                    lhsT_scale=x_scale[m][:, cols],
+                                    rhs=w_code[g][t][:].bitcast(FP8X4), rhs_scale=w_scale[g][t][:],
+                                    start=(g == 0), stop=(g == 1))
+            acc[(tau, t)] = ps
+
+        def rope(tau):
+            s, i = tau // 4, tau % 4
+            if i == 0:
+                o_tiles[s] = work.tile([P, 8, 4, P], F32, name="o_sb", tag="o_sb", bufs=3)
+            o_rope = o_tiles[s][:, :, i, 64:128]
+            x_hre = acc[(tau, ROPE)][:].rearrange("p (h r e) -> p h r e", h=8, e=2)
+            nc.vector.tensor_tensor(out=o_rope.rearrange("p h (r e) -> p h r e", e=2), in0=x_hre,
+                                    in1=cos_t[:, tau : tau + 1, :].unsqueeze(3).to_broadcast([P, 8, 32, 2]),
+                                    op=ALU.mult)
+            p2 = work.tile([P, 8, 64], F32, name="p2", tag="p2", bufs=4)
+            nc.vector.tensor_tensor(out=p2[:].rearrange("p h (r e) -> p h r e", e=2), in0=x_hre[:, :, :, ::-1],
+                                    in1=sin_t[:, tau : tau + 1, :, :].rearrange("p o e r -> p o r e").to_broadcast([P, 8, 32, 2]),
+                                    op=ALU.mult)
+            nc.gpsimd.tensor_tensor(out=o_rope, in0=o_rope, in1=p2[:], op=ALU.add)
+
+        def nope(tau):
+            s, i = tau // 4, tau % 4
+            nc.scalar.copy(out=o_tiles[s][:, :, i, 0:64], in_=acc[(tau, NOPE)][:].rearrange("p (h d) -> p h d", h=8))
+
+        def store0(s, h0, nh):
+            nc.sync.dma_start(
+                out=out_0[0, h0 : h0 + nh, 512 * s : 512 * (s + 1), :].rearrange("h (p i) d -> p h (i d)", i=4),
+                in_=o_tiles[s][:, h0 : h0 + nh].rearrange("p h i d -> p h (i d)"),
+            )
+
+        def store0_tile(tau):
+            s, i = tau // 4, tau % 4
+            nc.sync.dma_start(
+                out=out_0[0, :, 512 * s : 512 * (s + 1), :].rearrange("h (p i) d -> p h i d", i=4)[:, :, i, :],
+                in_=o_tiles[s][:, :, i, :],
+            )
+
+        def ep2(s, h0, nh, share):
+            o = o_tiles[s]
+            rows = 4 * nh
+            amax = work.tile([P, 16], F32, name="amax", tag="amax", bufs=4)
+            nc.vector.tensor_reduce(out=amax[:, 0:rows], in_=o[:, h0 : h0 + nh].rearrange("p h i d -> p (h i) d"),
+                                    axis=AX.X, op=ALU.max, apply_absolute_value=True)
+            rinv = work.tile([P, 16], F32, name="rinv", tag="rinv", bufs=4)
+            nc.vector.reciprocal(out=rinv[:, 0:rows], in_=amax[:, 0:rows])
+            fac = work.tile([P, 16], F32, name="fac", tag="fac", bufs=4)
+            nc.vector.tensor_scalar(out=fac[:, 0:rows], in0=rinv[:, 0:rows], scalar1=448.0, scalar2=None, op0=ALU.mult)
+            q = work.tile([P, 16, P], FP8, name="q_sb", tag="q_sb", bufs=4)
+            for r in range(rows):
+                row = o[:, h0 + r // 4, r % 4, :]
+                if share and r % 2 == 1:
+                    nc.vector.tensor_scalar(out=q[:, r, :], in0=row, scalar1=fac[:, r : r + 1], scalar2=None,
+                                            op0=ALU.mult, saturate=False)
+                else:
+                    nc.scalar.activation(out=q[:, r, :], in_=row, func=ACT.Identity,
+                                         bias=zero[:, 0:1], scale=fac[:, r : r + 1], saturate=False)
+            nc.sync.dma_start(
+                out=out_1[0, h0 : h0 + nh, 512 * s : 512 * (s + 1), :].rearrange("h (p i) d -> p h (i d)", i=4),
+                in_=q[:, 0:rows, :].bitcast(U8).rearrange("p (h i) d -> p h (i d)", h=nh),
+            )
+
+        with tc.manual_schedule(engines={mybir.EngineType.Activation, mybir.EngineType.DVE}):
+            nc.vector.memset(zero[:], 0.0)
+            nc.scalar.activation(out=warm[:], in_=zero[:], func=ACT.Sin)
+            nc.gpsimd.iota(tpos[:], pattern=[[512, 4], [1, 4]], base=0, channel_multiplier=4,
+                           allow_small_or_imprecise_dtypes=True)
+            make_identity(nc, ident[:])
+            frequencies()
+            reduced_angles(0, 4)
+            reduced_angles(4, 16)
+            cos_sin(0, 4)
+            transpose_pair(0)
+            interleave_w(0)
+            quant_w(0, ROPE)
+            quant_pair(0)
+            interleave_w(1)
+            quant_w(1, ROPE)
+            transpose_pair(1)
+        pending = []
+        served = 0
+        for m in range(8):
+            mm(2 * m, ROPE)
+            mm(2 * m + 1, ROPE)
+            if m == 0:
+                quant_w(0, NOPE)
+                quant_w(1, NOPE)
+                quant_pair(1)
+            mm(2 * m, NOPE)
+            mm(2 * m + 1, NOPE)
+            if m + 2 < 8:
+                transpose_pair(m + 2)
+            rope(2 * m)
+            nope(2 * m)
+            if m >= 6:
+                store0_tile(2 * m)
+            if served < len(pending) and m < 7:
+                ep2(*pending[served])
+                served += 1
+            rope(2 * m + 1)
+            nope(2 * m + 1)
+            if m >= 6:
+                store0_tile(2 * m + 1)
+            if m + 2 < 8:
+                quant_pair(m + 2)
+            if m == 0:
+                cos_sin(4, 16)
+            if m % 2 == 1 and m < 7:
+                s = m // 2
+                store0(s, 0, 4)
+                store0(s, 4, 4)
+                pending.append((s, 0, 4, False))
+                pending.append((s, 4, 4, False))
+        for item in pending[served:]:
+            ep2(*item)
+        ep2(3, 0, 2, False)
+        ep2(3, 2, 2, True)
+        ep2(3, 4, 2, True)
+        ep2(3, 6, 2, True)

@@ -164,7 +164,9 @@ def tile_deepseekv4attention_pb_kernel(tc, hidden, wq, out_0, out_1):
                                     start=(g == 0), stop=(g == 1))
             acc[(tau, t)] = ps
 
-        def rope(tau):
+        p2_tiles = {}
+
+        def rope_p1(tau):
             s, i = tau // 4, tau % 4
             if i == 0:
                 o_tiles[s] = work.tile([P, 8, 4, P], F32, name="o_sb", tag="o_sb", bufs=3)
@@ -173,6 +175,11 @@ def tile_deepseekv4attention_pb_kernel(tc, hidden, wq, out_0, out_1):
             nc.vector.tensor_tensor(out=o_rope.rearrange("p h (r e) -> p h r e", e=2), in0=x_hre,
                                     in1=cos_t[:, tau : tau + 1, :].unsqueeze(3).to_broadcast([P, 8, 32, 2]),
                                     op=ALU.mult)
+
+        def rope_p2(tau):
+            s, i = tau // 4, tau % 4
+            o_rope = o_tiles[s][:, :, i, 64:128]
+            x_hre = acc[(tau, ROPE)][:].rearrange("p (h r e) -> p h r e", h=8, e=2)
             p2 = work.tile([P, 8, 64], F32, name="p2", tag="p2", bufs=4)
             nc.vector.tensor_tensor(out=p2[:].rearrange("p h (r e) -> p h r e", e=2), in0=x_hre[:, :, :, ::-1],
                                     in1=sin_t[:, tau : tau + 1, :, :].rearrange("p o e r -> p o r e").to_broadcast([P, 8, 32, 2]),
@@ -196,31 +203,50 @@ def tile_deepseekv4attention_pb_kernel(tc, hidden, wq, out_0, out_1):
                 in_=o_tiles[s][:, :, i, :],
             )
 
-        def ep2(s, h0, nh, share):
-            o = o_tiles[s]
+        groups = {}
+
+        def reduce_rows(k, s, h0, nh, by_vector):
             rows = 4 * nh
-            amax = work.tile([P, 16], F32, name="amax", tag="amax", bufs=4)
-            nc.vector.tensor_reduce(out=amax[:, 0:rows], in_=o[:, h0 : h0 + nh].rearrange("p h i d -> p (h i) d"),
+            amax = work.tile([P, 16], F32, name="amax", tag="amax", bufs=6)
+            nc.vector.tensor_reduce(out=amax[:, 0:rows],
+                                    in_=o_tiles[s][:, h0 : h0 + nh].rearrange("p h i d -> p (h i) d"),
                                     axis=AX.X, op=ALU.max, apply_absolute_value=True)
-            rinv = work.tile([P, 16], F32, name="rinv", tag="rinv", bufs=4)
-            nc.vector.reciprocal(out=rinv[:, 0:rows], in_=amax[:, 0:rows])
-            fac = work.tile([P, 16], F32, name="fac", tag="fac", bufs=4)
-            nc.vector.tensor_scalar(out=fac[:, 0:rows], in0=rinv[:, 0:rows], scalar1=448.0, scalar2=None, op0=ALU.mult)
-            q = work.tile([P, 16, P], FP8, name="q_sb", tag="q_sb", bufs=4)
+            groups[k] = [s, h0, nh, by_vector, amax, None, None, None]
+
+        def recip_rows(k):
+            rows = 4 * groups[k][2]
+            rinv = work.tile([P, 16], F32, name="rinv", tag="rinv", bufs=6)
+            nc.vector.reciprocal(out=rinv[:, 0:rows], in_=groups[k][4][:, 0:rows])
+            fac = work.tile([P, 16], F32, name="fac", tag="fac", bufs=6)
+            nc.gpsimd.tensor_scalar(out=fac[:, 0:rows], in0=rinv[:, 0:rows], scalar1=448.0, scalar2=0.0,
+                                    op0=ALU.mult, op1=ALU.add)
+            groups[k][5] = fac
+
+        def cast_rows(k, engine):
+            s, h0, nh, by_vector, amax, fac, q, done = groups[k]
+            rows = 4 * nh
+            if q is None:
+                q = work.tile([P, 16, P], FP8, name="q_sb", tag="q_sb", bufs=6)
+                groups[k][6] = q
             for r in range(rows):
-                row = o[:, h0 + r // 4, r % 4, :]
-                if share and r % 2 == 1:
-                    nc.vector.tensor_scalar(out=q[:, r, :], in0=row, scalar1=fac[:, r : r + 1], scalar2=None,
-                                            op0=ALU.mult, saturate=False)
-                else:
+                row = o_tiles[s][:, h0 + r // 4, r % 4, :]
+                if r % 4 < by_vector:
+                    if engine == "vector":
+                        nc.vector.tensor_scalar(out=q[:, r, :], in0=row, scalar1=fac[:, r : r + 1], scalar2=None,
+                                                op0=ALU.mult, saturate=False)
+                elif engine == "scalar":
                     nc.scalar.activation(out=q[:, r, :], in_=row, func=ACT.Identity,
                                          bias=zero[:, 0:1], scale=fac[:, r : r + 1], saturate=False)
+
+        def store1(k):
+            s, h0, nh, by_vector, amax, fac, q, done = groups[k]
             nc.sync.dma_start(
                 out=out_1[0, h0 : h0 + nh, 512 * s : 512 * (s + 1), :].rearrange("h (p i) d -> p h (i d)", i=4),
-                in_=q[:, 0:rows, :].bitcast(U8).rearrange("p (h i) d -> p h (i d)", h=nh),
+                in_=q[:, 0 : 4 * nh, :].bitcast(U8).rearrange("p (h i) d -> p h (i d)", h=nh),
             )
 
-        with tc.manual_schedule(engines={mybir.EngineType.Activation, mybir.EngineType.DVE}):
+        with tc.manual_schedule(engines={mybir.EngineType.Activation, mybir.EngineType.DVE, mybir.EngineType.Pool,
+                                         mybir.EngineType.SP}):
             nc.vector.memset(zero[:], 0.0)
             nc.scalar.activation(out=warm[:], in_=zero[:], func=ACT.Sin)
             nc.gpsimd.iota(tpos[:], pattern=[[512, 4], [1, 4]], base=0, channel_multiplier=4,
@@ -237,43 +263,63 @@ def tile_deepseekv4attention_pb_kernel(tc, hidden, wq, out_0, out_1):
             interleave_w(1)
             quant_w(1, ROPE)
             transpose_pair(1)
-        pending = []
-        served = 0
-        for m in range(8):
-            mm(2 * m, ROPE)
-            mm(2 * m + 1, ROPE)
-            if m == 0:
-                quant_w(0, NOPE)
-                quant_w(1, NOPE)
-                quant_pair(1)
-            mm(2 * m, NOPE)
-            mm(2 * m + 1, NOPE)
-            if m + 2 < 8:
-                transpose_pair(m + 2)
-            rope(2 * m)
-            nope(2 * m)
-            if m >= 6:
-                store0_tile(2 * m)
-            if served < len(pending) and m < 7:
-                ep2(*pending[served])
-                served += 1
-            rope(2 * m + 1)
-            nope(2 * m + 1)
-            if m >= 6:
-                store0_tile(2 * m + 1)
-            if m + 2 < 8:
-                quant_pair(m + 2)
-            if m == 0:
-                cos_sin(4, 16)
-            if m % 2 == 1 and m < 7:
-                s = m // 2
-                store0(s, 0, 4)
-                store0(s, 4, 4)
-                pending.append((s, 0, 4, False))
-                pending.append((s, 4, 4, False))
-        for item in pending[served:]:
-            ep2(*item)
-        ep2(3, 0, 2, False)
-        ep2(3, 2, 2, True)
-        ep2(3, 4, 2, True)
-        ep2(3, 6, 2, True)
+            for m in range(8):
+                k_new = m - 2
+                k_old = m - 3
+                mm(2 * m, ROPE)
+                mm(2 * m + 1, ROPE)
+                if m == 0:
+                    quant_w(0, NOPE)
+                    quant_w(1, NOPE)
+                    quant_pair(1)
+                mm(2 * m, NOPE)
+                mm(2 * m + 1, NOPE)
+                if m + 2 < 8:
+                    transpose_pair(m + 2)
+                rope_p1(2 * m)
+                if k_old >= 0:
+                    recip_rows(k_old)
+                rope_p2(2 * m)
+                nope(2 * m)
+                if m >= 6:
+                    store0_tile(2 * m)
+                if k_old >= 0:
+                    cast_rows(k_old, "scalar")
+                    store1(k_old)
+                rope_p1(2 * m + 1)
+                rope_p2(2 * m + 1)
+                nope(2 * m + 1)
+                if m >= 6:
+                    store0_tile(2 * m + 1)
+                if k_new >= 0:
+                    reduce_rows(k_new, k_new // 2, 4 * (k_new % 2), 4, 0)
+                if m + 2 < 8:
+                    quant_pair(m + 2)
+                if m == 0:
+                    cos_sin(4, 8)
+                if m == 1:
+                    cos_sin(8, 16)
+                if m % 2 == 1 and m < 7:
+                    store0(m // 2, 0, 4)
+                    store0(m // 2, 4, 4)
+            reduce_rows(6, 3, 0, 2, 0)
+            recip_rows(5)
+            reduce_rows(7, 3, 2, 2, 4)
+            recip_rows(6)
+            reduce_rows(8, 3, 4, 2, 3)
+            recip_rows(7)
+            reduce_rows(9, 3, 6, 2, 2)
+            recip_rows(8)
+            cast_rows(5, "scalar")
+            store1(5)
+            cast_rows(6, "scalar")
+            store1(6)
+            cast_rows(7, "vector")
+            store1(7)
+            recip_rows(9)
+            cast_rows(8, "vector")
+            cast_rows(8, "scalar")
+            store1(8)
+            cast_rows(9, "vector")
+            cast_rows(9, "scalar")
+            store1(9)

@@ -134,12 +134,12 @@ def tile_deepseekv4attention_pb_kernel(tc, hidden, wq, out_0, out_1):
             for ch in range(2):
                 cols = slice(256 * ch, 256 * (ch + 1))
                 nc.vector.tensor_copy(
-                    out=w_grp[g][ROPE][:, cols, :].rearrange("q (h d) j -> q h d j", h=4),
-                    in_=w_raw[g][ch][:].rearrange("q j (h t d) -> q t h d j", h=4, t=2)[:, ROPE],
+                    out=w_grp[g][ROPE][:, cols, :].rearrange("q (h c i) j -> q h c j i", h=4, i=4),
+                    in_=w_raw[g][ch][:].rearrange("q j (h t c i) -> q t h c j i", h=4, t=2, i=4)[:, ROPE],
                 )
                 nc.scalar.copy(
-                    out=w_grp[g][NOPE][:, cols, :].rearrange("q (h d) j -> q h d j", h=4),
-                    in_=w_raw[g][ch][:].rearrange("q j (h t d) -> q t h d j", h=4, t=2)[:, NOPE],
+                    out=w_grp[g][NOPE][:, cols, :].rearrange("q (h c i) j -> q h c j i", h=4, i=4),
+                    in_=w_raw[g][ch][:].rearrange("q j (h t c i) -> q t h c j i", h=4, t=2, i=4)[:, NOPE],
                 )
 
         def quant_w(g, t):

@@ -245,8 +245,7 @@ def tile_deepseekv4attention_pb_kernel(tc, hidden, wq, out_0, out_1):
                 in_=q[:, 0 : 4 * nh, :].bitcast(U8).rearrange("p (h i) d -> p h (i d)", h=nh),
             )
 
-        with tc.manual_schedule(engines={mybir.EngineType.Activation, mybir.EngineType.DVE, mybir.EngineType.Pool,
-                                         mybir.EngineType.SP}):
+        with tc.manual_schedule():
             nc.vector.memset(zero[:], 0.0)
             nc.scalar.activation(out=warm[:], in_=zero[:], func=ACT.Sin)
             nc.gpsimd.iota(tpos[:], pattern=[[512, 4], [1, 4]], base=0, channel_multiplier=4,
@@ -257,12 +256,20 @@ def tile_deepseekv4attention_pb_kernel(tc, hidden, wq, out_0, out_1):
             reduced_angles(4, 16)
             cos_sin(0, 4)
             transpose_pair(0)
+            warm_ps = psum.tile([P, 512], F32, name="acc%d" % NOPE, tag="acc%d" % NOPE, bufs=3)
+            for g in range(2):
+                for ch in range(2):
+                    for j in (1, 2):
+                        nc.tensor.matmul(out=warm_ps[:], lhsT=w_raw[g][ch][:, 0, 0:P], rhs=w_raw[g][ch][:, j, :],
+                                         start=True, stop=True)
             interleave_w(0)
             quant_w(0, ROPE)
             quant_pair(0)
             interleave_w(1)
             quant_w(1, ROPE)
             transpose_pair(1)
+        with tc.manual_schedule(engines={mybir.EngineType.Activation, mybir.EngineType.DVE, mybir.EngineType.Pool,
+                                         mybir.EngineType.SP}):
             for m in range(8):
                 k_new = m - 2
                 k_old = m - 3

@@ -95,8 +95,8 @@ def tile_deepseekv4attention_pb_kernel(tc, hidden, wq, out_0, out_1):
                 nc.scalar.activation(out=half_sin[:, ph, cs, :], in_=red2[:, cs, :], func=ACT.Sin,
                                      bias=-0.25 * PI * ph, scale=0.5)
             nc.scalar.activation(out=half_sq[:, 0, cs, :], in_=half_sin[:, 0, cs, :], func=ACT.Square)
-            nc.scalar.activation(out=cos_t[:, cs, :], in_=half_sq[:, 0, cs, :], func=ACT.Copy, bias=1.0, scale=-2.0)
             nc.scalar.activation(out=half_sq[:, 1, cs, :], in_=half_sin[:, 1, cs, :], func=ACT.Square)
+            nc.scalar.activation(out=cos_t[:, cs, :], in_=half_sq[:, 0, cs, :], func=ACT.Copy, bias=1.0, scale=-2.0)
             nc.scalar.activation(out=sin_t[:, cs, 0, :], in_=half_sq[:, 1, cs, :], func=ACT.Copy, bias=-1.0, scale=2.0)
             nc.scalar.activation(out=sin_t[:, cs, 1, :], in_=half_sq[:, 1, cs, :], func=ACT.Copy, bias=1.0, scale=-2.0)
 
@@ -263,9 +263,10 @@ def tile_deepseekv4attention_pb_kernel(tc, hidden, wq, out_0, out_1):
                         nc.tensor.matmul(out=warm_ps[:], lhsT=w_raw[g][ch][:, 0, 0:P], rhs=w_raw[g][ch][:, j, :],
                                          start=True, stop=True)
             interleave_w(0)
-            quant_w(0, ROPE)
             quant_pair(0)
+            quant_w(0, ROPE)
             interleave_w(1)
+            quant_w(0, NOPE)
             quant_w(1, ROPE)
             transpose_pair(1)
         with tc.manual_schedule(engines={mybir.EngineType.Activation, mybir.EngineType.DVE, mybir.EngineType.Pool,
@@ -276,7 +277,6 @@ def tile_deepseekv4attention_pb_kernel(tc, hidden, wq, out_0, out_1):
                 mm(2 * m, ROPE)
                 mm(2 * m + 1, ROPE)
                 if m == 0:
-                    quant_w(0, NOPE)
                     quant_w(1, NOPE)
                     quant_pair(1)
                 mm(2 * m, NOPE)

@@ -309,7 +309,7 @@ def tile_deepseekv4attention_pb_kernel(tc, hidden, wq, out_0, out_1):
                 if m % 2 == 1 and m < 7:
                     store0(m // 2, 0, 4)
                     store0(m // 2, 4, 4)
-            reduce_rows(6, 3, 0, 2, 0)
+            reduce_rows(6, 3, 0, 2, 4)
             recip_rows(5)
             reduce_rows(7, 3, 2, 2, 4)
             recip_rows(6)
@@ -319,7 +319,7 @@ def tile_deepseekv4attention_pb_kernel(tc, hidden, wq, out_0, out_1):
             recip_rows(8)
             cast_rows(5, "scalar")
             store1(5)
-            cast_rows(6, "scalar")
+            cast_rows(6, "vector")
             store1(6)
             cast_rows(7, "vector")
             store1(7)

@@ -281,7 +281,7 @@ def tile_deepseekv4attention_pb_kernel(tc, hidden, wq, out_0, out_1):
                     quant_pair(1)
                 mm(2 * m, NOPE)
                 mm(2 * m + 1, NOPE)
-                if m + 2 < 8:
+                if m <= 2:
                     transpose_pair(m + 2)
                 rope_p1(2 * m)
                 if k_old >= 0:
@@ -302,6 +302,8 @@ def tile_deepseekv4attention_pb_kernel(tc, hidden, wq, out_0, out_1):
                     reduce_rows(k_new, k_new // 2, 4 * (k_new % 2), 4, 0)
                 if m + 2 < 8:
                     quant_pair(m + 2)
+                if 2 <= m <= 4:
+                    transpose_pair(m + 3)
                 if m == 0:
                     cos_sin(4, 8)
                 if m == 1:
@@ -309,7 +311,7 @@ def tile_deepseekv4attention_pb_kernel(tc, hidden, wq, out_0, out_1):
                 if m % 2 == 1 and m < 7:
                     store0(m // 2, 0, 4)
                     store0(m // 2, 4, 4)
-            reduce_rows(6, 3, 0, 2, 4)
+            reduce_rows(6, 3, 0, 2, 1)
             recip_rows(5)
             reduce_rows(7, 3, 2, 2, 4)
             recip_rows(6)
@@ -317,13 +319,14 @@ def tile_deepseekv4attention_pb_kernel(tc, hidden, wq, out_0, out_1):
             recip_rows(7)
             reduce_rows(9, 3, 6, 2, 2)
             recip_rows(8)
+            recip_rows(9)
             cast_rows(5, "scalar")
             store1(5)
             cast_rows(6, "vector")
+            cast_rows(6, "scalar")
             store1(6)
             cast_rows(7, "vector")
             store1(7)
-            recip_rows(9)
             cast_rows(8, "vector")
             cast_rows(8, "scalar")
             store1(8)

@@ -137,10 +137,16 @@ def tile_deepseekv4attention_pb_kernel(tc, hidden, wq, out_0, out_1):
                     out=w_grp[g][ROPE][:, cols, :].rearrange("q (h c i) j -> q h c j i", h=4, i=4),
                     in_=w_raw[g][ch][:].rearrange("q j (h t c i) -> q t h c j i", h=4, t=2, i=4)[:, ROPE],
                 )
-                nc.scalar.copy(
-                    out=w_grp[g][NOPE][:, cols, :].rearrange("q (h c i) j -> q h c j i", h=4, i=4),
-                    in_=w_raw[g][ch][:].rearrange("q j (h t c i) -> q t h c j i", h=4, t=2, i=4)[:, NOPE],
-                )
+                if (g, ch) == (1, 1):
+                    nc.vector.tensor_copy(
+                        out=w_grp[g][NOPE][:, cols, :].rearrange("q (h c i) j -> q h c j i", h=4, i=4),
+                        in_=w_raw[g][ch][:].rearrange("q j (h t c i) -> q t h c j i", h=4, t=2, i=4)[:, NOPE],
+                    )
+                else:
+                    nc.scalar.copy(
+                        out=w_grp[g][NOPE][:, cols, :].rearrange("q (h c i) j -> q h c j i", h=4, i=4),
+                        in_=w_raw[g][ch][:].rearrange("q j (h t c i) -> q t h c j i", h=4, t=2, i=4)[:, NOPE],
+                    )
 
         def quant_w(g, t):
             wc = const.tile([P, 512], U32, name="w_code%d%d" % (g, t), tag="w_code%d%d" % (g, t), align_bytes=64)
@@ -152,6 +158,7 @@ def tile_deepseekv4attention_pb_kernel(tc, hidden, wq, out_0, out_1):
 
         acc = {}
         o_tiles = {}
+        q_tiles = {}
 
         def mm(tau, t):
             m, a = tau // 2, tau % 2
@@ -164,21 +171,19 @@ def tile_deepseekv4attention_pb_kernel(tc, hidden, wq, out_0, out_1):
                                     start=(g == 0), stop=(g == 1))
             acc[(tau, t)] = ps
 
-        p2_tiles = {}
-
         def rope_p1(tau):
-            s, i = tau // 4, tau % 4
-            if i == 0:
-                o_tiles[s] = work.tile([P, 8, 4, P], F32, name="o_sb", tag="o_sb", bufs=3)
-            o_rope = o_tiles[s][:, :, i, 64:128]
+            m, a = tau // 2, tau % 2
+            if a == 0:
+                o_tiles[m] = work.tile([P, 8, 2, P], F32, name="o_sb", tag="o_sb", bufs=5)
+            o_rope = o_tiles[m][:, :, a, 64:128]
             x_hre = acc[(tau, ROPE)][:].rearrange("p (h r e) -> p h r e", h=8, e=2)
             nc.vector.tensor_tensor(out=o_rope.rearrange("p h (r e) -> p h r e", e=2), in0=x_hre,
                                     in1=cos_t[:, tau : tau + 1, :].unsqueeze(3).to_broadcast([P, 8, 32, 2]),
                                     op=ALU.mult)
 
         def rope_p2(tau):
-            s, i = tau // 4, tau % 4
-            o_rope = o_tiles[s][:, :, i, 64:128]
+            m, a = tau // 2, tau % 2
+            o_rope = o_tiles[m][:, :, a, 64:128]
             x_hre = acc[(tau, ROPE)][:].rearrange("p (h r e) -> p h r e", h=8, e=2)
             p2 = work.tile([P, 8, 64], F32, name="p2", tag="p2", bufs=4)
             nc.vector.tensor_tensor(out=p2[:].rearrange("p h (r e) -> p h r e", e=2), in0=x_hre[:, :, :, ::-1],
@@ -187,62 +192,55 @@ def tile_deepseekv4attention_pb_kernel(tc, hidden, wq, out_0, out_1):
             nc.gpsimd.tensor_tensor(out=o_rope, in0=o_rope, in1=p2[:], op=ALU.add)
 
         def nope(tau):
-            s, i = tau // 4, tau % 4
-            nc.scalar.copy(out=o_tiles[s][:, :, i, 0:64], in_=acc[(tau, NOPE)][:].rearrange("p (h d) -> p h d", h=8))
+            m, a = tau // 2, tau % 2
+            nc.scalar.copy(out=o_tiles[m][:, :, a, 0:64], in_=acc[(tau, NOPE)][:].rearrange("p (h d) -> p h d", h=8))
 
-        def store0(s, h0, nh):
+        def store0(m, h0, nh):
+            s = m // 2
             nc.sync.dma_start(
-                out=out_0[0, h0 : h0 + nh, 512 * s : 512 * (s + 1), :].rearrange("h (p i) d -> p h (i d)", i=4),
-                in_=o_tiles[s][:, h0 : h0 + nh].rearrange("p h i d -> p h (i d)"),
-            )
-
-        def store0_tile(tau):
-            s, i = tau // 4, tau % 4
-            nc.sync.dma_start(
-                out=out_0[0, :, 512 * s : 512 * (s + 1), :].rearrange("h (p i) d -> p h i d", i=4)[:, :, i, :],
-                in_=o_tiles[s][:, :, i, :],
+                out=out_0[0, h0 : h0 + nh, 512 * s : 512 * (s + 1), :].rearrange("h (p j i) d -> j p h (i d)", j=2, i=2)[m % 2],
+                in_=o_tiles[m][:, h0 : h0 + nh].rearrange("p h i d -> p h (i d)"),
             )
 
         groups = {}
 
-        def reduce_rows(k, s, h0, nh, by_vector):
-            rows = 4 * nh
+        def reduce_rows(k, m, h0, nh):
+            rows = 2 * nh
             amax = work.tile([P, 16], F32, name="amax", tag="amax", bufs=6)
             nc.vector.tensor_reduce(out=amax[:, 0:rows],
-                                    in_=o_tiles[s][:, h0 : h0 + nh].rearrange("p h i d -> p (h i) d"),
+                                    in_=o_tiles[m][:, h0 : h0 + nh].rearrange("p h i d -> p (h i) d"),
                                     axis=AX.X, op=ALU.max, apply_absolute_value=True)
-            groups[k] = [s, h0, nh, by_vector, amax, None, None, None]
+            groups[k] = [m, h0, nh, amax, None]
 
         def recip_rows(k):
-            rows = 4 * groups[k][2]
+            rows = 2 * groups[k][2]
             rinv = work.tile([P, 16], F32, name="rinv", tag="rinv", bufs=6)
-            nc.vector.reciprocal(out=rinv[:, 0:rows], in_=groups[k][4][:, 0:rows])
+            nc.vector.reciprocal(out=rinv[:, 0:rows], in_=groups[k][3][:, 0:rows])
             fac = work.tile([P, 16], F32, name="fac", tag="fac", bufs=6)
             nc.gpsimd.tensor_scalar(out=fac[:, 0:rows], in0=rinv[:, 0:rows], scalar1=448.0, scalar2=0.0,
                                     op0=ALU.mult, op1=ALU.add)
-            groups[k][5] = fac
+            groups[k][4] = fac
 
-        def cast_rows(k, engine):
-            s, h0, nh, by_vector, amax, fac, q, done = groups[k]
-            rows = 4 * nh
-            if q is None:
-                q = work.tile([P, 16, P], FP8, name="q_sb", tag="q_sb", bufs=6)
-                groups[k][6] = q
-            for r in range(rows):
-                row = o_tiles[s][:, h0 + r // 4, r % 4, :]
-                if r % 4 < by_vector:
-                    if engine == "vector":
-                        nc.vector.tensor_scalar(out=q[:, r, :], in0=row, scalar1=fac[:, r : r + 1], scalar2=None,
-                                                op0=ALU.mult, saturate=False)
-                elif engine == "scalar":
-                    nc.scalar.activation(out=q[:, r, :], in_=row, func=ACT.Identity,
+        def cast_rows(k, engine, r0, r1):
+            m, h0, nh, amax, fac = groups[k]
+            s = m // 2
+            if s not in q_tiles:
+                q_tiles[s] = work.tile([P, 8, 4, P], FP8, name="q_sb", tag="q_sb", bufs=2)
+            for r in range(r0, r1):
+                h, a = h0 + r // 2, r % 2
+                row = o_tiles[m][:, h, a, :]
+                q_row = q_tiles[s][:, h, 2 * (m % 2) + a, :]
+                if engine == "vector":
+                    nc.vector.tensor_scalar(out=q_row, in0=row, scalar1=fac[:, r : r + 1], scalar2=None,
+                                            op0=ALU.mult, saturate=False)
+                else:
+                    nc.scalar.activation(out=q_row, in_=row, func=ACT.Identity,
                                          bias=zero[:, 0:1], scale=fac[:, r : r + 1], saturate=False)
 
-        def store1(k):
-            s, h0, nh, by_vector, amax, fac, q, done = groups[k]
+        def store1(s, h0, nh):
             nc.sync.dma_start(
                 out=out_1[0, h0 : h0 + nh, 512 * s : 512 * (s + 1), :].rearrange("h (p i) d -> p h (i d)", i=4),
-                in_=q[:, 0 : 4 * nh, :].bitcast(U8).rearrange("p (h i) d -> p h (i d)", h=nh),
+                in_=q_tiles[s][:, h0 : h0 + nh].bitcast(U8).rearrange("p h i d -> p h (i d)"),
             )
 
         with tc.manual_schedule():
@@ -272,8 +270,6 @@ def tile_deepseekv4attention_pb_kernel(tc, hidden, wq, out_0, out_1):
         with tc.manual_schedule(engines={mybir.EngineType.Activation, mybir.EngineType.DVE, mybir.EngineType.Pool,
                                          mybir.EngineType.SP}):
             for m in range(8):
-                k_new = m - 2
-                k_old = m - 3
                 mm(2 * m, ROPE)
                 mm(2 * m + 1, ROPE)
                 if m == 0:
@@ -284,22 +280,22 @@ def tile_deepseekv4attention_pb_kernel(tc, hidden, wq, out_0, out_1):
                 if m <= 2:
                     transpose_pair(m + 2)
                 rope_p1(2 * m)
-                if k_old >= 0:
-                    recip_rows(k_old)
+                if m >= 2:
+                    recip_rows(m - 2)
                 rope_p2(2 * m)
                 nope(2 * m)
-                if m >= 6:
-                    store0_tile(2 * m)
-                if k_old >= 0:
-                    cast_rows(k_old, "scalar")
-                    store1(k_old)
+                if m >= 2:
+                    cast_rows(m - 2, "scalar", 0, 16)
+                    if m % 2 == 1:
+                        store1((m - 2) // 2, 0, 4)
+                        store1((m - 2) // 2, 4, 4)
                 rope_p1(2 * m + 1)
                 rope_p2(2 * m + 1)
                 nope(2 * m + 1)
-                if m >= 6:
-                    store0_tile(2 * m + 1)
-                if k_new >= 0:
-                    reduce_rows(k_new, k_new // 2, 4 * (k_new % 2), 4, 0)
+                store0(m, 0, 4)
+                store0(m, 4, 4)
+                if m >= 1:
+                    reduce_rows(m - 1, m - 1, 0, 8)
                 if m + 2 < 8:
                     quant_pair(m + 2)
                 if 2 <= m <= 4:
@@ -308,28 +304,15 @@ def tile_deepseekv4attention_pb_kernel(tc, hidden, wq, out_0, out_1):
                     cos_sin(4, 8)
                 if m == 1:
                     cos_sin(8, 16)
-                if m % 2 == 1 and m < 7:
-                    store0(m // 2, 0, 4)
-                    store0(m // 2, 4, 4)
-            reduce_rows(6, 3, 0, 2, 1)
-            recip_rows(5)
-            reduce_rows(7, 3, 2, 2, 4)
             recip_rows(6)
-            reduce_rows(8, 3, 4, 2, 3)
+            reduce_rows(7, 7, 0, 4)
+            reduce_rows(8, 7, 4, 4)
             recip_rows(7)
-            reduce_rows(9, 3, 6, 2, 2)
             recip_rows(8)
-            recip_rows(9)
-            cast_rows(5, "scalar")
-            store1(5)
-            cast_rows(6, "vector")
-            cast_rows(6, "scalar")
-            store1(6)
-            cast_rows(7, "vector")
-            store1(7)
-            cast_rows(8, "vector")
-            cast_rows(8, "scalar")
-            store1(8)
-            cast_rows(9, "vector")
-            cast_rows(9, "scalar")
-            store1(9)
+            cast_rows(6, "scalar", 0, 16)
+            cast_rows(7, "vector", 0, 5)
+            cast_rows(7, "scalar", 5, 8)
+            store1(3, 0, 4)
+            cast_rows(8, "vector", 0, 5)
+            cast_rows(8, "scalar", 5, 8)
+            store1(3, 4, 4)

@@ -23,6 +23,14 @@ FREQ_RATIO = 10000.0 ** (-1.0 / 32.0)
 PI = 3.141592653589793
 TWO_PI_HI = 6.28125
 TWO_PI_LO = 2.0 * PI - TWO_PI_HI
+ROOT2 = 2.0 ** 0.5
+HALF_PHASE = (0.0, -0.375 * PI, -0.125 * PI)
+TAB_SCALE = (-2.0, -2.0 * ROOT2, 2.0 * ROOT2)
+TAB_BIAS = (1.0, ROOT2, -ROOT2)
+FOUR_PRODUCT_TILES = 4
+HALF_PHASE_4 = (0.0, -0.25 * PI, -0.25 * PI)
+TAB_SCALE_4 = (-2.0, -2.0, 2.0)
+TAB_BIAS_4 = (1.0, 1.0, -1.0)
 
 
 def tile_deepseekv4attention_pb_kernel(tc, hidden, wq, out_0, out_1):
@@ -66,10 +74,9 @@ def tile_deepseekv4attention_pb_kernel(tc, hidden, wq, out_0, out_1):
         turns = const.tile([P, 16, 32], I32, name="turns", tag="turns")
         red1 = const.tile([P, 16, 32], F32, name="red1", tag="red1")
         red2 = const.tile([P, 16, 32], F32, name="red2", tag="red2")
-        half_sin = const.tile([P, 2, 16, 32], F32, name="half_sin", tag="half_sin")
-        half_sq = const.tile([P, 2, 16, 32], F32, name="half_sq", tag="half_sq")
-        cos_t = const.tile([P, 16, 32], F32, name="cos_t", tag="cos_t")
-        sin_t = const.tile([P, 16, 2, 32], F32, name="sin_t", tag="sin_t")
+        half_sin = const.tile([P, 3, 16, 32], F32, name="half_sin", tag="half_sin")
+        half_sq = const.tile([P, 3, 16, 32], F32, name="half_sq", tag="half_sq")
+        tab = const.tile([P, 3, 16, 32], F32, name="tab", tag="tab")
 
         def frequencies():
             nc.vector.memset(freq[:, 0:1], 1.0)
@@ -89,16 +96,30 @@ def tile_deepseekv4attention_pb_kernel(tc, hidden, wq, out_0, out_1):
             nc.vector.scalar_tensor_tensor(out=red2[:, cs, :], in0=turns[:, cs, :], scalar=-TWO_PI_LO,
                                            in1=red1[:, cs, :], op0=ALU.mult, op1=ALU.add)
 
-        def cos_sin(c0, c1):
+        def half_sines(c0, c1, phase):
+            cs = slice(c0, c1)
+            for ph in range(3):
+                nc.scalar.activation(out=half_sin[:, ph, cs, :], in_=red2[:, cs, :], func=ACT.Sin,
+                                     bias=phase[ph], scale=0.5)
+
+        def tables_by_scalar(c0, c1):
+            cs = slice(c0, c1)
+            for ph in range(3):
+                nc.scalar.activation(out=half_sq[:, ph, cs, :], in_=half_sin[:, ph, cs, :], func=ACT.Square)
+            for ph in range(3):
+                nc.scalar.activation(out=tab[:, ph, cs, :], in_=half_sq[:, ph, cs, :], func=ACT.Copy,
+                                     bias=TAB_BIAS[ph], scale=TAB_SCALE[ph])
+
+        def four_product_tables(c0, c1):
             cs = slice(c0, c1)
             for ph in range(2):
                 nc.scalar.activation(out=half_sin[:, ph, cs, :], in_=red2[:, cs, :], func=ACT.Sin,
-                                     bias=-0.25 * PI * ph, scale=0.5)
-            nc.scalar.activation(out=half_sq[:, 0, cs, :], in_=half_sin[:, 0, cs, :], func=ACT.Square)
-            nc.scalar.activation(out=half_sq[:, 1, cs, :], in_=half_sin[:, 1, cs, :], func=ACT.Square)
-            nc.scalar.activation(out=cos_t[:, cs, :], in_=half_sq[:, 0, cs, :], func=ACT.Copy, bias=1.0, scale=-2.0)
-            nc.scalar.activation(out=sin_t[:, cs, 0, :], in_=half_sq[:, 1, cs, :], func=ACT.Copy, bias=-1.0, scale=2.0)
-            nc.scalar.activation(out=sin_t[:, cs, 1, :], in_=half_sq[:, 1, cs, :], func=ACT.Copy, bias=1.0, scale=-2.0)
+                                     bias=HALF_PHASE_4[ph], scale=0.5)
+            for ph in range(2):
+                nc.scalar.activation(out=half_sq[:, ph, cs, :], in_=half_sin[:, ph, cs, :], func=ACT.Square)
+            for ph in range(3):
+                nc.scalar.activation(out=tab[:, ph, cs, :], in_=half_sq[:, min(ph, 1), cs, :], func=ACT.Copy,
+                                     bias=TAB_BIAS_4[ph], scale=TAB_SCALE_4[ph])
 
         x_grp = {}
         x_code = {}
@@ -133,10 +154,11 @@ def tile_deepseekv4attention_pb_kernel(tc, hidden, wq, out_0, out_1):
                                          align_bytes=64)
             for ch in range(2):
                 cols = slice(256 * ch, 256 * (ch + 1))
-                nc.vector.tensor_copy(
-                    out=w_grp[g][ROPE][:, cols, :].rearrange("q (h c i) j -> q h c j i", h=4, i=4),
-                    in_=w_raw[g][ch][:].rearrange("q j (h t c i) -> q t h c j i", h=4, t=2, i=4)[:, ROPE],
-                )
+                for e in range(2):
+                    nc.vector.tensor_copy(
+                        out=w_grp[g][ROPE][:].rearrange("q (e x h c i) j -> q x e h c j i", e=2, x=2, h=4, i=4)[:, ch, e],
+                        in_=w_raw[g][ch][:].rearrange("q j (h t c i e) -> q t e h c j i", h=4, t=2, i=4, e=2)[:, ROPE, e],
+                    )
                 if (g, ch) == (1, 1):
                     nc.vector.tensor_copy(
                         out=w_grp[g][NOPE][:, cols, :].rearrange("q (h c i) j -> q h c j i", h=4, i=4),
@@ -160,36 +182,68 @@ def tile_deepseekv4attention_pb_kernel(tc, hidden, wq, out_0, out_1):
         o_tiles = {}
         q_tiles = {}
 
-        def mm(tau, t):
-            m, a = tau // 2, tau % 2
-            ps = psum.tile([P, 512], F32, name="acc%d" % t, tag="acc%d" % t, bufs=3)
-            for g in range(2):
-                cols = slice(256 * a + 128 * g, 256 * a + 128 * (g + 1))
-                nc.tensor.matmul_mx(out=ps[:], lhsT=x_code[m][:, cols].bitcast(FP8X4),
-                                    lhsT_scale=x_scale[m][:, cols],
-                                    rhs=w_code[g][t][:].bitcast(FP8X4), rhs_scale=w_scale[g][t][:],
-                                    start=(g == 0), stop=(g == 1))
-            acc[(tau, t)] = ps
+        sums = {}
+        mixes = {}
 
-        def rope_p1(tau):
+        def x_cols(a, g):
+            return slice(256 * a + 128 * g, 256 * a + 128 * (g + 1))
+
+        def mm_nope(tau):
+            m, a = tau // 2, tau % 2
+            ps = psum.tile([P, 512], F32, name="acc_n", tag="acc_n", bufs=2)
+            for g in range(2):
+                nc.tensor.matmul_mx(out=ps[:], lhsT=x_code[m][:, x_cols(a, g)].bitcast(FP8X4),
+                                    lhsT_scale=x_scale[m][:, x_cols(a, g)],
+                                    rhs=w_code[g][NOPE][:].bitcast(FP8X4), rhs_scale=w_scale[g][NOPE][:],
+                                    start=(g == 0), stop=(g == 1))
+            acc[(tau, NOPE)] = ps
+
+        def mm_rope(tau):
+            m, a = tau // 2, tau % 2
+            ps = psum.tile([P, 512], F32, name="acc_r", tag="acc_r", bufs=2)
+            if a == 0 and tau >= FOUR_PRODUCT_TILES:
+                sums[m] = psum.tile([P, 512], F32, name="acc_s", tag="acc_s", bufs=2)
+            for g in range(2):
+                nc.tensor.matmul_mx(out=ps[:], lhsT=x_code[m][:, x_cols(a, g)].bitcast(FP8X4),
+                                    lhsT_scale=x_scale[m][:, x_cols(a, g)],
+                                    rhs=w_code[g][ROPE][:].bitcast(FP8X4), rhs_scale=w_scale[g][ROPE][:],
+                                    start=(g == 0), stop=(g == 1))
+                for e in range(2 if tau >= FOUR_PRODUCT_TILES else 0):
+                    half = slice(256 * e, 256 * (e + 1))
+                    nc.tensor.matmul_mx(out=sums[m][:, 256 * a : 256 * (a + 1)],
+                                        lhsT=x_code[m][:, x_cols(a, g)].bitcast(FP8X4),
+                                        lhsT_scale=x_scale[m][:, x_cols(a, g)],
+                                        rhs=w_code[g][ROPE][:, half].bitcast(FP8X4), rhs_scale=w_scale[g][ROPE][:, half],
+                                        start=(g == 0 and e == 0), stop=(g == 1 and e == 1))
+            acc[(tau, ROPE)] = ps
+
+        def rope_mix(tau):
             m, a = tau // 2, tau % 2
             if a == 0:
                 o_tiles[m] = work.tile([P, 8, 2, P], F32, name="o_sb", tag="o_sb", bufs=5)
-            o_rope = o_tiles[m][:, :, a, 64:128]
-            x_hre = acc[(tau, ROPE)][:].rearrange("p (h r e) -> p h r e", h=8, e=2)
-            nc.vector.tensor_tensor(out=o_rope.rearrange("p h (r e) -> p h r e", e=2), in0=x_hre,
-                                    in1=cos_t[:, tau : tau + 1, :].unsqueeze(3).to_broadcast([P, 8, 32, 2]),
-                                    op=ALU.mult)
+            mix = work.tile([P, 512], F32, name="mix", tag="mix", bufs=4)
+            nc.vector.tensor_tensor(out=mix[:].rearrange("p (e h r) -> p e h r", e=2, h=8),
+                                    in0=acc[(tau, ROPE)][:].rearrange("p (e h r) -> p e h r", e=2, h=8),
+                                    in1=tab[:, 1:3, tau : tau + 1, :].to_broadcast([P, 2, 8, 32]), op=ALU.mult)
+            mixes[tau] = mix
 
-        def rope_p2(tau):
+        def rope_common(tau):
             m, a = tau // 2, tau % 2
-            o_rope = o_tiles[m][:, :, a, 64:128]
-            x_hre = acc[(tau, ROPE)][:].rearrange("p (h r e) -> p h r e", h=8, e=2)
-            p2 = work.tile([P, 8, 64], F32, name="p2", tag="p2", bufs=4)
-            nc.vector.tensor_tensor(out=p2[:].rearrange("p h (r e) -> p h r e", e=2), in0=x_hre[:, :, :, ::-1],
-                                    in1=sin_t[:, tau : tau + 1, :, :].rearrange("p o e r -> p o r e").to_broadcast([P, 8, 32, 2]),
-                                    op=ALU.mult)
-            nc.gpsimd.tensor_tensor(out=o_rope, in0=o_rope, in1=p2[:], op=ALU.add)
+            com = work.tile([P, 512], F32, name="com", tag="com", bufs=4)
+            if tau >= FOUR_PRODUCT_TILES:
+                nc.vector.tensor_tensor(out=com[:, 0:256].rearrange("p (h r) -> p h r", h=8),
+                                        in0=sums[m][:, 256 * a : 256 * (a + 1)].rearrange("p (h r) -> p h r", h=8),
+                                        in1=tab[:, 0, tau : tau + 1, :].to_broadcast([P, 8, 32]), op=ALU.mult)
+                first = com[:, 0:256].rearrange("p (h r) -> p h r", h=8).unsqueeze(3).to_broadcast([P, 8, 32, 2])
+            else:
+                nc.vector.tensor_tensor(out=com[:].rearrange("p (x r) -> p x r", r=32),
+                                        in0=acc[(tau, ROPE)][:].rearrange("p (x r) -> p x r", r=32),
+                                        in1=tab[:, 0, tau : tau + 1, :].to_broadcast([P, 16, 32]), op=ALU.mult)
+                first = com[:].rearrange("p (e h r) -> p h r e", e=2, h=8)
+            nc.gpsimd.tensor_tensor(out=o_tiles[m][:, :, a, 64:128].rearrange("p h (r e) -> p h r e", e=2),
+                                    in0=first,
+                                    in1=mixes[tau][:].rearrange("p (e h r) -> p h r e", e=2, h=8)[:, :, :, ::-1],
+                                    op=ALU.add)
 
         def nope(tau):
             m, a = tau // 2, tau % 2
@@ -252,9 +306,9 @@ def tile_deepseekv4attention_pb_kernel(tc, hidden, wq, out_0, out_1):
             frequencies()
             reduced_angles(0, 4)
             reduced_angles(4, 16)
-            cos_sin(0, 4)
+            four_product_tables(0, 4)
             transpose_pair(0)
-            warm_ps = psum.tile([P, 512], F32, name="acc%d" % NOPE, tag="acc%d" % NOPE, bufs=3)
+            warm_ps = psum.tile([P, 512], F32, name="acc_n", tag="acc_n", bufs=2)
             for g in range(2):
                 for ch in range(2):
                     for j in (1, 2):
@@ -270,27 +324,27 @@ def tile_deepseekv4attention_pb_kernel(tc, hidden, wq, out_0, out_1):
         with tc.manual_schedule(engines={mybir.EngineType.Activation, mybir.EngineType.DVE, mybir.EngineType.Pool,
                                          mybir.EngineType.SP}):
             for m in range(8):
-                mm(2 * m, ROPE)
-                mm(2 * m + 1, ROPE)
+                mm_rope(2 * m)
+                mm_rope(2 * m + 1)
                 if m == 0:
                     quant_w(1, NOPE)
                     quant_pair(1)
-                mm(2 * m, NOPE)
-                mm(2 * m + 1, NOPE)
+                mm_nope(2 * m)
+                mm_nope(2 * m + 1)
                 if m <= 2:
                     transpose_pair(m + 2)
-                rope_p1(2 * m)
+                rope_mix(2 * m)
                 if m >= 2:
                     recip_rows(m - 2)
-                rope_p2(2 * m)
+                rope_common(2 * m)
                 nope(2 * m)
                 if m >= 2:
                     cast_rows(m - 2, "scalar", 0, 16)
                     if m % 2 == 1:
                         store1((m - 2) // 2, 0, 4)
                         store1((m - 2) // 2, 4, 4)
-                rope_p1(2 * m + 1)
-                rope_p2(2 * m + 1)
+                rope_mix(2 * m + 1)
+                rope_common(2 * m + 1)
                 nope(2 * m + 1)
                 store0(m, 0, 4)
                 store0(m, 4, 4)
@@ -301,9 +355,11 @@ def tile_deepseekv4attention_pb_kernel(tc, hidden, wq, out_0, out_1):
                 if 2 <= m <= 4:
                     transpose_pair(m + 3)
                 if m == 0:
-                    cos_sin(4, 8)
+                    half_sines(4, 8, HALF_PHASE)
+                    tables_by_scalar(4, 8)
                 if m == 1:
-                    cos_sin(8, 16)
+                    half_sines(8, 16, HALF_PHASE)
+                    tables_by_scalar(8, 16)
             recip_rows(6)
             reduce_rows(7, 7, 0, 4)
             reduce_rows(8, 7, 4, 4)

@@ -334,10 +334,13 @@ def tile_deepseekv4attention_pb_kernel(tc, hidden, wq, out_0, out_1):
                 if m <= 2:
                     transpose_pair(m + 2)
                 rope_mix(2 * m)
+                if 1 <= m <= 6:
+                    quant_pair(m + 1)
                 if m >= 2:
                     recip_rows(m - 2)
                 rope_common(2 * m)
                 nope(2 * m)
+                nope(2 * m + 1)
                 if m >= 2:
                     cast_rows(m - 2, "scalar", 0, 16)
                     if m % 2 == 1:
@@ -345,13 +348,10 @@ def tile_deepseekv4attention_pb_kernel(tc, hidden, wq, out_0, out_1):
                         store1((m - 2) // 2, 4, 4)
                 rope_mix(2 * m + 1)
                 rope_common(2 * m + 1)
-                nope(2 * m + 1)
                 store0(m, 0, 4)
                 store0(m, 4, 4)
                 if m >= 1:
                     reduce_rows(m - 1, m - 1, 0, 8)
-                if m + 2 < 8:
-                    quant_pair(m + 2)
                 if 2 <= m <= 4:
                     transpose_pair(m + 3)
                 if m == 0:
@@ -366,9 +366,13 @@ def tile_deepseekv4attention_pb_kernel(tc, hidden, wq, out_0, out_1):
             recip_rows(7)
             recip_rows(8)
             cast_rows(6, "scalar", 0, 16)
-            cast_rows(7, "vector", 0, 5)
-            cast_rows(7, "scalar", 5, 8)
-            store1(3, 0, 4)
-            cast_rows(8, "vector", 0, 5)
-            cast_rows(8, "scalar", 5, 8)
-            store1(3, 4, 4)
+            cast_rows(7, "vector", 0, 4)
+            store1(3, 0, 2)
+            cast_rows(7, "vector", 4, 6)
+            cast_rows(7, "scalar", 6, 8)
+            store1(3, 2, 2)
+            cast_rows(8, "vector", 0, 4)
+            store1(3, 4, 2)
+            cast_rows(8, "vector", 4, 6)
+            cast_rows(8, "scalar", 6, 8)
+            store1(3, 6, 2)

@@ -271,8 +271,7 @@ def tile_deepseekv4attention_pb_kernel(tc, hidden, wq, out_0, out_1):
             rinv = work.tile([P, 16], F32, name="rinv", tag="rinv", bufs=6)
             nc.vector.reciprocal(out=rinv[:, 0:rows], in_=groups[k][3][:, 0:rows])
             fac = work.tile([P, 16], F32, name="fac", tag="fac", bufs=6)
-            nc.gpsimd.tensor_scalar(out=fac[:, 0:rows], in0=rinv[:, 0:rows], scalar1=448.0, scalar2=0.0,
-                                    op0=ALU.mult, op1=ALU.add)
+            nc.scalar.activation(out=fac[:, 0:rows], in_=rinv[:, 0:rows], func=ACT.Copy, scale=448.0)
             groups[k][4] = fac
 
         def cast_rows(k, engine, r0, r1):
@@ -331,7 +330,7 @@ def tile_deepseekv4attention_pb_kernel(tc, hidden, wq, out_0, out_1):
                     quant_pair(1)
                 mm_nope(2 * m)
                 mm_nope(2 * m + 1)
-                if m <= 2:
+                if m <= 5:
                     transpose_pair(m + 2)
                 rope_mix(2 * m)
                 if 1 <= m <= 6:
@@ -352,8 +351,6 @@ def tile_deepseekv4attention_pb_kernel(tc, hidden, wq, out_0, out_1):
                 store0(m, 4, 4)
                 if m >= 1:
                     reduce_rows(m - 1, m - 1, 0, 8)
-                if 2 <= m <= 4:
-                    transpose_pair(m + 3)
                 if m == 0:
                     half_sines(4, 8, HALF_PHASE)
                     tables_by_scalar(4, 8)
@@ -361,11 +358,11 @@ def tile_deepseekv4attention_pb_kernel(tc, hidden, wq, out_0, out_1):
                     half_sines(8, 16, HALF_PHASE)
                     tables_by_scalar(8, 16)
             recip_rows(6)
+            cast_rows(6, "scalar", 0, 16)
             reduce_rows(7, 7, 0, 4)
             reduce_rows(8, 7, 4, 4)
             recip_rows(7)
             recip_rows(8)
-            cast_rows(6, "scalar", 0, 16)
             cast_rows(7, "vector", 0, 4)
             store1(3, 0, 2)
             cast_rows(7, "vector", 4, 6)

@@ -320,18 +320,17 @@ def tile_deepseekv4attention_pb_kernel(tc, hidden, wq, out_0, out_1):
             quant_w(0, NOPE)
             quant_w(1, ROPE)
             transpose_pair(1)
-        with tc.manual_schedule(engines={mybir.EngineType.Activation, mybir.EngineType.DVE, mybir.EngineType.Pool,
-                                         mybir.EngineType.SP}):
+        with tc.manual_schedule():
             for m in range(8):
                 mm_rope(2 * m)
                 mm_rope(2 * m + 1)
                 if m == 0:
                     quant_w(1, NOPE)
                     quant_pair(1)
-                mm_nope(2 * m)
-                mm_nope(2 * m + 1)
                 if m <= 5:
                     transpose_pair(m + 2)
+                mm_nope(2 * m)
+                mm_nope(2 * m + 1)
                 rope_mix(2 * m)
                 if 1 <= m <= 6:
                     quant_pair(m + 1)

from contextlib import ExitStack

import concourse.mybir as mybir
from concourse.masks import make_identity

FLOPS = 2 * 2048 * 1024 * 1024

F32 = mybir.dt.float32
BF16 = mybir.dt.bfloat16
U32 = mybir.dt.uint32
I32 = mybir.dt.int32
U8 = mybir.dt.uint8
FP8X4 = mybir.dt.float8_e4m3fn_x4
FP8 = mybir.dt.float8_e4m3fn
ALU = mybir.AluOpType
ACT = mybir.ActivationFunctionType
AX = mybir.AxisListType

P = 128
NOPE = 0
ROPE = 1
FREQ_RATIO = 10000.0 ** (-1.0 / 32.0)
PI = 3.141592653589793
TWO_PI_HI = 6.28125
TWO_PI_LO = 2.0 * PI - TWO_PI_HI
ROOT2 = 2.0 ** 0.5
HALF_PHASE = (0.0, -0.375 * PI, -0.125 * PI)
TAB_SCALE = (-2.0, -2.0 * ROOT2, 2.0 * ROOT2)
TAB_BIAS = (1.0, ROOT2, -ROOT2)
FOUR_PRODUCT_TILES = 4
HALF_PHASE_4 = (0.0, -0.25 * PI, -0.25 * PI)
TAB_SCALE_4 = (-2.0, -2.0, 2.0)
TAB_BIAS_4 = (1.0, 1.0, -1.0)


def tile_deepseekv4attention_pb_kernel(tc, hidden, wq, out_0, out_1):
    nc = tc.nc
    with ExitStack() as ctx:
        const = ctx.enter_context(tc.tile_pool(name="const", bufs=1))
        work = ctx.enter_context(tc.tile_pool(name="work", bufs=3))
        psum = ctx.enter_context(tc.psum_pool(name="psum", bufs=2))

        hid = hidden.rearrange("b (s p i) k -> (b s) p i k", p=P, i=4)
        x_raw = []
        w_raw = [[None, None], [None, None]]

        def load_x(m):
            xr = const.tile([P, 2, 1024], BF16, name="x_raw%d" % m, tag="x_raw%d" % m)
            nc.sync.dma_start(out=xr[:], in_=hid[m // 2, :, 2 * (m % 2) : 2 * (m % 2) + 2, :])
            x_raw.append(xr)

        def load_w(g, ch):
            wr = const.tile([P, 4, 512], BF16, name="w_raw%d%d" % (g, ch), tag="w_raw%d%d" % (g, ch))
            nc.sync.dma_start(
                out=wr[:],
                in_=wq[512 * g : 512 * (g + 1), 512 * ch : 512 * (ch + 1)].rearrange("(q j) n -> q j n", j=4),
            )
            w_raw[g][ch] = wr

        load_x(0)
        load_w(0, 0)
        load_w(0, 1)
        load_w(1, 0)
        load_w(1, 1)
        for m in range(1, 8):
            load_x(m)

        zero = const.tile([P, 1], F32, name="zero", tag="zero")
        warm = const.tile([P, 1], F32, name="warm", tag="warm")
        ident = const.tile([P, P], F32, name="ident", tag="ident")
        tpos = const.tile([P, 16], F32, name="tpos", tag="tpos")
        freq = const.tile([P, 32], F32, name="freq", tag="freq")
        ang = const.tile([P, 16, 32], F32, name="ang", tag="ang")
        turns = const.tile([P, 16, 32], I32, name="turns", tag="turns")
        red1 = const.tile([P, 16, 32], F32, name="red1", tag="red1")
        red2 = const.tile([P, 16, 32], F32, name="red2", tag="red2")
        half_sin = const.tile([P, 3, 16, 32], F32, name="half_sin", tag="half_sin")
        half_sq = const.tile([P, 3, 16, 32], F32, name="half_sq", tag="half_sq")
        tab = const.tile([P, 3, 16, 32], F32, name="tab", tag="tab")

        def frequencies():
            nc.vector.memset(freq[:, 0:1], 1.0)
            for b in range(5):
                n = 1 << b
                nc.vector.tensor_scalar(out=freq[:, n : 2 * n], in0=freq[:, 0:n], scalar1=FREQ_RATIO ** n,
                                        scalar2=None, op0=ALU.mult)

        def reduced_angles(c0, c1):
            cs = slice(c0, c1)
            nc.vector.tensor_tensor(out=ang[:, cs, :], in0=tpos[:, cs].unsqueeze(2).to_broadcast([P, c1 - c0, 32]),
                                    in1=freq[:].unsqueeze(1).to_broadcast([P, c1 - c0, 32]), op=ALU.mult)
            nc.vector.tensor_scalar(out=turns[:, cs, :], in0=ang[:, cs, :], scalar1=1.0 / (2.0 * PI), scalar2=None,
                                    op0=ALU.mult)
            nc.vector.scalar_tensor_tensor(out=red1[:, cs, :], in0=turns[:, cs, :], scalar=-TWO_PI_HI,
                                           in1=ang[:, cs, :], op0=ALU.mult, op1=ALU.add)
            nc.vector.scalar_tensor_tensor(out=red2[:, cs, :], in0=turns[:, cs, :], scalar=-TWO_PI_LO,
                                           in1=red1[:, cs, :], op0=ALU.mult, op1=ALU.add)

        def half_sines(c0, c1, phase):
            cs = slice(c0, c1)
            for ph in range(3):
                nc.scalar.activation(out=half_sin[:, ph, cs, :], in_=red2[:, cs, :], func=ACT.Sin,
                                     bias=phase[ph], scale=0.5)

        def tables_by_scalar(c0, c1):
            cs = slice(c0, c1)
            for ph in range(3):
                nc.scalar.activation(out=half_sq[:, ph, cs, :], in_=half_sin[:, ph, cs, :], func=ACT.Square)
            for ph in range(3):
                nc.scalar.activation(out=tab[:, ph, cs, :], in_=half_sq[:, ph, cs, :], func=ACT.Copy,
                                     bias=TAB_BIAS[ph], scale=TAB_SCALE[ph])

        def four_product_tables(c0, c1):
            cs = slice(c0, c1)
            for ph in range(2):
                nc.scalar.activation(out=half_sin[:, ph, cs, :], in_=red2[:, cs, :], func=ACT.Sin,
                                     bias=HALF_PHASE_4[ph], scale=0.5)
            for ph in range(2):
                nc.scalar.activation(out=half_sq[:, ph, cs, :], in_=half_sin[:, ph, cs, :], func=ACT.Square)
            for ph in range(3):
                nc.scalar.activation(out=tab[:, ph, cs, :], in_=half_sq[:, min(ph, 1), cs, :], func=ACT.Copy,
                                     bias=TAB_BIAS_4[ph], scale=TAB_SCALE_4[ph])

        x_grp = {}
        x_code = {}
        x_scale = {}

        def transpose_pair(m):
            xg = work.tile([P, 2, 2, P, 4], BF16, name="x_grp", tag="x_grp", bufs=3, align_bytes=64)
            for a in range(2):
                words = x_raw[m][:, a, :].bitcast(F32)
                xt = psum.tile([P, 2, 2, P], F32, name="xt", tag="xt", bufs=2)
                for g in range(2):
                    for u in range(2):
                        nc.tensor.transpose(xt[:, g, u, :], words[:, 256 * g + u : 256 * (g + 1) : 2], ident[:])
                nc.scalar.copy(out=xg[:, a].bitcast(F32), in_=xt[:].rearrange("q g u p -> q g p u"))
            x_grp[m] = xg

        def quant_pair(m):
            xc = work.tile([P, 512], U32, name="x_code", tag="x_code", bufs=4, align_bytes=64)
            xs = work.tile([P, 512], U8, name="x_scale", tag="x_scale", bufs=4, align_bytes=64)
            nc.vector.quantize_mx(out=xc[:].bitcast(FP8X4), scales=xs[:],
                                  in_=x_grp[m][:].rearrange("q a g p t -> q (a g p t)"))
            x_code[m] = xc
            x_scale[m] = xs

        w_grp = [[None, None], [None, None]]
        w_code = [[None, None], [None, None]]
        w_scale = [[None, None], [None, None]]

        def interleave_w(g):
            for t in (ROPE, NOPE):
                w_grp[g][t] = const.tile([P, 512, 4], BF16, name="w_grp%d%d" % (g, t), tag="w_grp%d%d" % (g, t),
                                         align_bytes=64)
            for ch in range(2):
                cols = slice(256 * ch, 256 * (ch + 1))
                for e in range(2):
                    nc.vector.tensor_copy(
                        out=w_grp[g][ROPE][:].rearrange("q (e x h c i) j -> q x e h c j i", e=2, x=2, h=4, i=4)[:, ch, e],
                        in_=w_raw[g][ch][:].rearrange("q j (h t c i e) -> q t e h c j i", h=4, t=2, i=4, e=2)[:, ROPE, e],
                    )
                if (g, ch) == (1, 1):
                    nc.vector.tensor_copy(
                        out=w_grp[g][NOPE][:, cols, :].rearrange("q (h c i) j -> q h c j i", h=4, i=4),
                        in_=w_raw[g][ch][:].rearrange("q j (h t c i) -> q t h c j i", h=4, t=2, i=4)[:, NOPE],
                    )
                else:
                    nc.scalar.copy(
                        out=w_grp[g][NOPE][:, cols, :].rearrange("q (h c i) j -> q h c j i", h=4, i=4),
                        in_=w_raw[g][ch][:].rearrange("q j (h t c i) -> q t h c j i", h=4, t=2, i=4)[:, NOPE],
                    )

        def quant_w(g, t):
            wc = const.tile([P, 512], U32, name="w_code%d%d" % (g, t), tag="w_code%d%d" % (g, t), align_bytes=64)
            ws = const.tile([P, 512], U8, name="w_scale%d%d" % (g, t), tag="w_scale%d%d" % (g, t), align_bytes=64)
            nc.vector.quantize_mx(out=wc[:].bitcast(FP8X4), scales=ws[:],
                                  in_=w_grp[g][t][:].rearrange("q n j -> q (n j)"))
            w_code[g][t] = wc
            w_scale[g][t] = ws

        acc = {}
        o_tiles = {}
        q_tiles = {}

        sums = {}
        mixes = {}

        def x_cols(a, g):
            return slice(256 * a + 128 * g, 256 * a + 128 * (g + 1))

        def mm_nope(tau):
            m, a = tau // 2, tau % 2
            ps = psum.tile([P, 512], F32, name="acc_n", tag="acc_n", bufs=2)
            for g in range(2):
                nc.tensor.matmul_mx(out=ps[:], lhsT=x_code[m][:, x_cols(a, g)].bitcast(FP8X4),
                                    lhsT_scale=x_scale[m][:, x_cols(a, g)],
                                    rhs=w_code[g][NOPE][:].bitcast(FP8X4), rhs_scale=w_scale[g][NOPE][:],
                                    start=(g == 0), stop=(g == 1))
            acc[(tau, NOPE)] = ps

        def mm_rope(tau):
            m, a = tau // 2, tau % 2
            ps = psum.tile([P, 512], F32, name="acc_r", tag="acc_r", bufs=2)
            if a == 0 and tau >= FOUR_PRODUCT_TILES:
                sums[m] = psum.tile([P, 512], F32, name="acc_s", tag="acc_s", bufs=2)
            for g in range(2):
                nc.tensor.matmul_mx(out=ps[:], lhsT=x_code[m][:, x_cols(a, g)].bitcast(FP8X4),
                                    lhsT_scale=x_scale[m][:, x_cols(a, g)],
                                    rhs=w_code[g][ROPE][:].bitcast(FP8X4), rhs_scale=w_scale[g][ROPE][:],
                                    start=(g == 0), stop=(g == 1))
                for e in range(2 if tau >= FOUR_PRODUCT_TILES else 0):
                    half = slice(256 * e, 256 * (e + 1))
                    nc.tensor.matmul_mx(out=sums[m][:, 256 * a : 256 * (a + 1)],
                                        lhsT=x_code[m][:, x_cols(a, g)].bitcast(FP8X4),
                                        lhsT_scale=x_scale[m][:, x_cols(a, g)],
                                        rhs=w_code[g][ROPE][:, half].bitcast(FP8X4), rhs_scale=w_scale[g][ROPE][:, half],
                                        start=(g == 0 and e == 0), stop=(g == 1 and e == 1))
            acc[(tau, ROPE)] = ps

        def rope_mix(tau):
            m, a = tau // 2, tau % 2
            if a == 0:
                o_tiles[m] = work.tile([P, 8, 2, P], F32, name="o_sb", tag="o_sb", bufs=5)
            mix = work.tile([P, 512], F32, name="mix", tag="mix", bufs=4)
            nc.vector.tensor_tensor(out=mix[:].rearrange("p (e h r) -> p e h r", e=2, h=8),
                                    in0=acc[(tau, ROPE)][:].rearrange("p (e h r) -> p e h r", e=2, h=8),
                                    in1=tab[:, 1:3, tau : tau + 1, :].to_broadcast([P, 2, 8, 32]), op=ALU.mult)
            mixes[tau] = mix

        def rope_common(tau):
            m, a = tau // 2, tau % 2
            com = work.tile([P, 512], F32, name="com", tag="com", bufs=4)
            if tau >= FOUR_PRODUCT_TILES:
                nc.vector.tensor_tensor(out=com[:, 0:256].rearrange("p (h r) -> p h r", h=8),
                                        in0=sums[m][:, 256 * a : 256 * (a + 1)].rearrange("p (h r) -> p h r", h=8),
                                        in1=tab[:, 0, tau : tau + 1, :].to_broadcast([P, 8, 32]), op=ALU.mult)
                first = com[:, 0:256].rearrange("p (h r) -> p h r", h=8).unsqueeze(3).to_broadcast([P, 8, 32, 2])
            else:
                nc.vector.tensor_tensor(out=com[:].rearrange("p (x r) -> p x r", r=32),
                                        in0=acc[(tau, ROPE)][:].rearrange("p (x r) -> p x r", r=32),
                                        in1=tab[:, 0, tau : tau + 1, :].to_broadcast([P, 16, 32]), op=ALU.mult)
                first = com[:].rearrange("p (e h r) -> p h r e", e=2, h=8)
            nc.gpsimd.tensor_tensor(out=o_tiles[m][:, :, a, 64:128].rearrange("p h (r e) -> p h r e", e=2),
                                    in0=first,
                                    in1=mixes[tau][:].rearrange("p (e h r) -> p h r e", e=2, h=8)[:, :, :, ::-1],
                                    op=ALU.add)

        def nope(tau):
            m, a = tau // 2, tau % 2
            nc.scalar.copy(out=o_tiles[m][:, :, a, 0:64], in_=acc[(tau, NOPE)][:].rearrange("p (h d) -> p h d", h=8))

        def store0(m, h0, nh):
            s = m // 2
            nc.sync.dma_start(
                out=out_0[0, h0 : h0 + nh, 512 * s : 512 * (s + 1), :].rearrange("h (p j i) d -> j p h (i d)", j=2, i=2)[m % 2],
                in_=o_tiles[m][:, h0 : h0 + nh].rearrange("p h i d -> p h (i d)"),
            )

        groups = {}

        def reduce_rows(k, m, h0, nh):
            rows = 2 * nh
            amax = work.tile([P, 16], F32, name="amax", tag="amax", bufs=6)
            nc.vector.tensor_reduce(out=amax[:, 0:rows],
                                    in_=o_tiles[m][:, h0 : h0 + nh].rearrange("p h i d -> p (h i) d"),
                                    axis=AX.X, op=ALU.max, apply_absolute_value=True)
            groups[k] = [m, h0, nh, amax, None]

        def recip_rows(k):
            rows = 2 * groups[k][2]
            rinv = work.tile([P, 16], F32, name="rinv", tag="rinv", bufs=6)
            nc.vector.reciprocal(out=rinv[:, 0:rows], in_=groups[k][3][:, 0:rows])
            fac = work.tile([P, 16], F32, name="fac", tag="fac", bufs=6)
            nc.scalar.activation(out=fac[:, 0:rows], in_=rinv[:, 0:rows], func=ACT.Copy, scale=448.0)
            groups[k][4] = fac

        def cast_rows(k, engine, r0, r1):
            m, h0, nh, amax, fac = groups[k]
            s = m // 2
            if s not in q_tiles:
                q_tiles[s] = work.tile([P, 8, 4, P], FP8, name="q_sb", tag="q_sb", bufs=2)
            for r in range(r0, r1):
                h, a = h0 + r // 2, r % 2
                row = o_tiles[m][:, h, a, :]
                q_row = q_tiles[s][:, h, 2 * (m % 2) + a, :]
                if engine == "vector":
                    nc.vector.tensor_scalar(out=q_row, in0=row, scalar1=fac[:, r : r + 1], scalar2=None,
                                            op0=ALU.mult, saturate=False)
                else:
                    nc.scalar.activation(out=q_row, in_=row, func=ACT.Identity,
                                         bias=zero[:, 0:1], scale=fac[:, r : r + 1], saturate=False)

        def store1(s, h0, nh):
            nc.sync.dma_start(
                out=out_1[0, h0 : h0 + nh, 512 * s : 512 * (s + 1), :].rearrange("h (p i) d -> p h (i d)", i=4),
                in_=q_tiles[s][:, h0 : h0 + nh].bitcast(U8).rearrange("p h i d -> p h (i d)"),
            )

        with tc.manual_schedule():
            nc.vector.memset(zero[:], 0.0)
            nc.scalar.activation(out=warm[:], in_=zero[:], func=ACT.Sin)
            nc.gpsimd.iota(tpos[:], pattern=[[512, 4], [1, 4]], base=0, channel_multiplier=4,
                           allow_small_or_imprecise_dtypes=True)
            make_identity(nc, ident[:])
            frequencies()
            reduced_angles(0, 4)
            reduced_angles(4, 16)
            four_product_tables(0, 4)
            transpose_pair(0)
            warm_ps = psum.tile([P, 512], F32, name="acc_n", tag="acc_n", bufs=2)
            for g in range(2):
                for ch in range(2):
                    for j in (1, 2):
                        nc.tensor.matmul(out=warm_ps[:], lhsT=w_raw[g][ch][:, 0, 0:P], rhs=w_raw[g][ch][:, j, :],
                                         start=True, stop=True)
            interleave_w(0)
            quant_pair(0)
            quant_w(0, ROPE)
            interleave_w(1)
            quant_w(0, NOPE)
            quant_w(1, ROPE)
            transpose_pair(1)
        with tc.manual_schedule():
            for m in range(8):
                mm_rope(2 * m)
                mm_rope(2 * m + 1)
                if m == 0:
                    quant_w(1, NOPE)
                    quant_pair(1)
                if m <= 5:
                    transpose_pair(m + 2)
                mm_nope(2 * m)
                mm_nope(2 * m + 1)
                rope_mix(2 * m)
                if 1 <= m <= 6:
                    quant_pair(m + 1)
                if m >= 2:
                    recip_rows(m - 2)
                rope_common(2 * m)
                nope(2 * m)
                nope(2 * m + 1)
                if m >= 2:
                    cast_rows(m - 2, "scalar", 0, 16)
                    if m % 2 == 1:
                        store1((m - 2) // 2, 0, 4)
                        store1((m - 2) // 2, 4, 4)
                rope_mix(2 * m + 1)
                rope_common(2 * m + 1)
                store0(m, 0, 4)
                store0(m, 4, 4)
                if m >= 1:
                    reduce_rows(m - 1, m - 1, 0, 8)
                if m == 0:
                    half_sines(4, 8, HALF_PHASE)
                    tables_by_scalar(4, 8)
                if m == 1:
                    half_sines(8, 16, HALF_PHASE)
                    tables_by_scalar(8, 16)
            recip_rows(6)
            cast_rows(6, "scalar", 0, 16)
            reduce_rows(7, 7, 0, 4)
            reduce_rows(8, 7, 4, 4)
            recip_rows(7)
            recip_rows(8)
            cast_rows(7, "vector", 0, 4)
            store1(3, 0, 2)
            cast_rows(7, "vector", 4, 6)
            cast_rows(7, "scalar", 6, 8)
            store1(3, 2, 2)
            cast_rows(8, "vector", 0, 4)
            store1(3, 4, 2)
            cast_rows(8, "vector", 4, 6)
            cast_rows(8, "scalar", 6, 8)
            store1(3, 6, 2)
